import numpy as np
import ml_dtypes


def mxq(x, axis, fmt="e4m3"):
    dtype, down = {"e4m3": (ml_dtypes.float8_e4m3fn, 7), "e5m2": (ml_dtypes.float8_e5m2, 14)}[fmt]
    v = np.moveaxis(np.asarray(x, np.float32).astype(ml_dtypes.bfloat16).astype(np.float64), axis, -1)
    blocks = v.reshape(v.shape[:-1] + (-1, 32))
    amax = np.abs(blocks).max(-1, keepdims=True)
    byte = np.maximum(np.where(amax > 0, np.frexp(amax)[1] - 1 + 127, 0) - down, 1)
    scale = np.exp2(byte - 127.0)
    codes = (blocks / scale).astype(np.float32).astype(dtype).astype(np.float64)
    return np.moveaxis((codes * scale).reshape(v.shape), -1, axis)


WIDE = False


def mx_kscale(k):
    if not WIDE:
        return np.ones(k)
    levels = np.array([10, -10, 5, -5, 0])
    if k % 512:
        return np.exp2(np.random.permutation(np.resize(levels, k // 32))).repeat(32)
    a = np.empty((k // 512, 16))
    for p in range(k // 512):
        a[p, :8] = np.random.permutation(np.resize(levels, 8))
        for g in range(8):
            far = levels[np.abs(levels - a[p, g]) >= 10]
            a[p, g + 8] = far[np.random.randint(len(far))]
    return np.exp2(a.ravel()).repeat(32)


BF16 = ml_dtypes.bfloat16


def bf(x):
    return np.asarray(x, np.float32).astype(BF16)


def f64(x):
    return np.asarray(x).astype(np.float64)


B, CIN, P, COUT, W, H, HEADS = 2, 1024, 512, 2048, 16, 32, 4
N = W * H
T = B * N
EPS = 1e-5


def bn(y, g, b, m, v):
    return (y - f64(m)[None, :, None]) * (f64(g) / np.sqrt(f64(v) + EPS))[None, :, None] + f64(b)[None, :, None]


def pre_relu(h_attn, x, conv3_w, bn3_g, bn3_b, bn3_m, bn3_v, sc_w, sc_b, scbn_g, scbn_b, scbn_m, scbn_v):
    main = bn(f64(conv3_w) @ f64(h_attn), bn3_g, bn3_b, bn3_m, bn3_v)
    short = bn(f64(sc_w) @ f64(x) + f64(sc_b)[None, :, None], scbn_g, scbn_b, scbn_m, scbn_v)
    return main + short


def setup_inputs():
    s = mx_kscale(T).reshape(B, 1, N)
    u = mx_kscale(COUT)
    h_attn = bf(np.maximum(np.random.standard_normal((B, P, N)), 0.0))
    x0 = bf(np.random.standard_normal((B, CIN, N)))
    conv3_w = bf(np.random.standard_normal((COUT, P)) * 1.5 / np.sqrt(P))
    bn3_g = bf(np.random.uniform(0.5, 1.5, COUT))
    bn3_b = bf(np.random.standard_normal(COUT) * 0.3)
    bn3_m = bf(np.random.standard_normal(COUT) * 0.3)
    bn3_v = bf(np.random.uniform(0.5, 1.5, COUT))
    sc_w0 = bf(np.random.standard_normal((COUT, CIN)) / np.sqrt(CIN))
    sc_b = bf(np.random.standard_normal(COUT) * 0.3)
    scbn_g = bf(np.random.uniform(0.5, 1.5, COUT))
    scbn_b = bf(np.random.standard_normal(COUT) * 0.3)
    scbn_m = bf(np.random.standard_normal(COUT) * 0.3)
    scbn_v = bf(np.random.uniform(0.5, 1.5, COUT))
    g = bf(np.random.standard_normal((B, COUT, N)) * np.exp2(np.random.randint(-6, 1, (B, 1, N))) * 2.0 / s * u[None, :, None])
    z = pre_relu(h_attn, x0, conv3_w, bn3_g, bn3_b, bn3_m, bn3_v, sc_w0, sc_b, scbn_g, scbn_b, scbn_m, scbn_v)
    return {
        "h_attn": h_attn,
        "x": bf(f64(x0) * s),
        "conv3_w": conv3_w,
        "bn3_g": bn3_g,
        "bn3_b": bn3_b,
        "bn3_m": bn3_m,
        "bn3_v": bn3_v,
        "sc_w": bf(f64(sc_w0) / u[:, None]),
        "sc_b": sc_b,
        "scbn_g": scbn_g,
        "scbn_b": scbn_b,
        "scbn_m": scbn_m,
        "scbn_v": scbn_v,
        "z": np.asarray(z, np.float32),
        "grad_out": g,
    }


def reference(h_attn, x, conv3_w, bn3_g, bn3_b, bn3_m, bn3_v, sc_w, sc_b, scbn_g, scbn_b, scbn_m, scbn_v, z, grad_out):
    a = f64(scbn_g) / np.sqrt(f64(scbn_v) + EPS)
    dz = f64(grad_out) * np.where(f64(z) > 0.0, 1.0, 0.0) * a[None, :, None]
    dx = mxq(f64(sc_w), 0, "e4m3").T @ mxq(dz, 1, "e5m2")
    dz2 = dz.transpose(1, 0, 2).reshape(COUT, T)
    x2 = f64(x).transpose(1, 0, 2).reshape(CIN, T)
    dw = mxq(dz2, 1, "e5m2") @ mxq(x2, 1, "e4m3").T
    return dx, dw

@@ -1,0 +1,284 @@
+from contextlib import ExitStack
+
+import concourse.mybir as mybir
+from concourse.masks import make_identity
+
+B, CIN, COUT, N = 2, 1024, 2048, 512
+EPS = 1e-5
+
+F32 = mybir.dt.float32
+BF16 = mybir.dt.bfloat16
+U32 = mybir.dt.uint32
+U8 = mybir.dt.uint8
+E4 = mybir.dt.float8_e4m3fn_x4
+E5 = mybir.dt.float8_e5m2_x4
+ALU = mybir.AluOpType
+ACT = mybir.ActivationFunctionType
+
+P = 128
+PACK = 4
+KP = P * PACK
+G = COUT // KP
+IT = CIN // P
+
+FLOPS = 2 * 2 * COUT * CIN * B * N
+BYTES = 2 * (B * CIN * N + COUT * CIN + B * COUT * N + 2 * COUT) + 4 * (B * COUT * N + B * CIN * N + COUT * CIN)
+
+ORDER = [(0, 0), (1, 0), (2, 0), (3, 0), (0, 1), (1, 1), (2, 1), (3, 1)]
+
+RUN = [
+    ("gv",), ("Lh", 0, 0), ("Lh", 0, 1), ("LW", 0), ("L", 1), ("LW", 1),
+    ("L", 2), ("LW", 2), ("L", 3), ("a1",), ("sqrt",), ("a2",),
+    ("maskh", 0, 0), ("maskh", 0, 1), ("scale", 0), ("weave", 0), ("turn", 0), ("wi", 0, 0, "S"),
+    ("unturn", 0), ("wi", 0, 1, "S"), ("mask", 1), ("wi", 0, 2, "S"), ("wi", 0, 3, "S"), ("wi", 1, 0, "S"),
+    ("LW", 3), ("wq", 0), ("wi", 1, 1, "S"), ("qb", 0), ("scale", 1), ("wi", 1, 2, "S"),
+    ("qa", 0), ("turn", 1), ("weave", 1), ("wi", 1, 3, "S"), ("m0", 0, 0, (0,)), ("m0", 0, 1, (0,)),
+    ("m0", 0, 2, (0,)), ("unturn", 1), ("mask", 2), ("LX", 0), ("L", 4), ("m0", 0, 3, (0,)),
+    ("m0", 0, 4, (0,)), ("m0", 0, 5, (0,)), ("wi", 2, 0, "S"), ("wq", 1), ("wi", 2, 1, "S"), ("qb", 1),
+    ("wi", 2, 2, "S"), ("scale", 2), ("wi", 2, 3, "S"), ("qa", 1), ("turn", 2), ("weave", 2),
+    ("unturn", 2), ("LX", 1), ("L", 5), ("m0", 0, 0, (1,)), ("L", 6), ("m0", 0, 1, (1,)),
+    ("mask", 3), ("m0", 0, 2, (1,)), ("wi", 3, 0, "S"), ("m0", 0, 3, (1,)), ("m0", 0, 4, (1,)), ("m0", 0, 5, (1,)),
+    ("wi", 3, 1, "S"), ("xt", 0, 0), ("wq", 2), ("L", 7), ("wi", 3, 2, "S"), ("xt", 0, 1),
+    ("qb", 2), ("xc", 0, 0), ("scale", 3), ("xc", 0, 1), ("xt", 0, 2), ("wi", 3, 3, "S"),
+    ("qa", 2), ("xt", 0, 3), ("weave", 3), ("xc", 0, 2), ("xc", 0, 3), ("turn", 3),
+    ("xq", 0), ("unturn", 3), ("m0", 0, 0, (2,)), ("m0", 0, 1, (2,)), ("mask", 4), ("m0", 0, 2, (2,)),
+    ("m0", 0, 3, (2,)), ("m0", 0, 4, (2,)), ("m0", 0, 5, (2,)), ("xt", 1, 0), ("xt", 1, 1), ("wq", 3),
+    ("qb", 3), ("xc", 1, 0), ("scale", 4), ("xc", 1, 1), ("xt", 1, 2), ("xt", 1, 3),
+    ("qa", 3), ("xc", 1, 2), ("xc", 1, 3), ("turn", 4), ("xq", 1), ("unturn", 4),
+    ("m0", 0, 0, (3,)), ("m0", 0, 1, (3,)), ("mask", 5), ("m0", 0, 2, (3,)), ("o0", 0, 0, "S"), ("m0", 0, 3, (3,)),
+    ("m0", 0, 4, (3,)), ("o0", 0, 1, "S"), ("s0", 0, 0), ("m0", 0, 5, (3,)), ("m0", 0, 6, (0,1,2,3)), ("o0", 0, 2, "S"),
+    ("s0", 0, 1), ("o0", 0, 3, "S"), ("s0", 0, 2), ("scale", 5), ("m0", 0, 7, (0,1,2,3)), ("s0", 0, 3),
+    ("qb", 4), ("turn", 5), ("o0", 0, 4, "S"), ("mask", 6), ("o0", 0, 5, "S"), ("s0", 0, 4),
+    ("m1", 0, 0), ("unturn", 5), ("s0", 0, 5), ("m1", 0, 1), ("o0", 0, 6, "S"), ("m1", 0, 2),
+    ("scale", 6), ("o0", 0, 7, "S"), ("m1", 0, 3), ("s0", 0, 6), ("qb", 5), ("o1", 0, 0, "S"),
+    ("turn", 6), ("s0", 0, 7), ("weave", 4), ("o1", 0, 1, "S"), ("unturn", 6), ("m1", 0, 4),
+    ("mask", 7), ("m1", 0, 5), ("o1", 0, 2, "S"), ("m1", 0, 6), ("o1", 0, 3, "S"), ("m1", 0, 7),
+    ("o1", 0, 4, "S"), ("s1", 0, 0), ("m1", 1, 0), ("qa", 4), ("o1", 0, 5, "S"), ("m1", 1, 1),
+    ("o1", 0, 6, "S"), ("scale", 7), ("m1", 1, 2), ("o1", 0, 7, "S"), ("m1", 1, 3), ("qb", 6),
+    ("o1", 1, 0, "S"), ("s1", 0, 1), ("turn", 7), ("weave", 5), ("o1", 1, 1, "S"), ("unturn", 7),
+    ("m1", 1, 4), ("qa", 5), ("m1", 1, 5), ("o1", 1, 2, "S"), ("qb", 7), ("m1", 1, 6),
+    ("o1", 1, 3, "S"), ("weave", 6), ("m1", 1, 7), ("o1", 1, 4, "S"), ("s1", 1, 0), ("m1", 2, 0),
+    ("o1", 1, 5, "S"), ("m1", 2, 1), ("qa", 6), ("o1", 1, 6, "S"), ("m1", 2, 2), ("weave", 7),
+    ("o1", 1, 7, "S"), ("m1", 2, 3), ("o1", 2, 0, "S"), ("s1", 1, 1), ("m1", 2, 4), ("o1", 2, 1, "S"),
+    ("qa", 7), ("m1", 2, 5), ("o1", 2, 2, "S"), ("m1", 2, 6), ("o1", 2, 3, "S"), ("m1", 2, 7),
+    ("s1", 2, 0), ("o1", 2, 4, "S"), ("m1", 3, 0), ("o1", 2, 5, "S"), ("m1", 3, 1), ("o1", 2, 6, "S"),
+    ("m1", 3, 2), ("o1", 2, 7, "S"), ("m1", 3, 3), ("o1", 3, 0, "S"), ("s1", 2, 1), ("m1", 3, 4),
+    ("o1", 3, 1, "S"), ("m1", 3, 5), ("o1", 3, 2, "S"), ("m1", 3, 6), ("o1", 3, 3, "S"), ("m1", 3, 7),
+    ("o1", 3, 4, "S"), ("s1", 3, 0), ("m0", 1, 0, (0,1,2,3)), ("o1", 3, 5, "S"), ("o1", 3, 6, "S"), ("m0", 1, 1, (0,1,2,3)),
+    ("o1", 3, 7, "S"), ("o0", 1, 0, "S"), ("s1", 3, 1), ("m0", 1, 2, (0,1,2,3)), ("o0", 1, 1, "V"), ("s0", 1, 0),
+    ("s0", 1, 1), ("m0", 1, 3, (0,1,2,3)), ("o0", 1, 2, "S"), ("s0", 1, 2), ("m0", 1, 4, (0,1,2,3)), ("o0", 1, 3, "V"),
+    ("s0", 1, 3), ("m0", 1, 5, (0,1,2,3)), ("m0", 1, 6, (0,1,2,3)), ("o0", 1, 5, "V"), ("o0", 1, 4, "S"), ("m0", 1, 7, (0,1,2,3)),
+    ("o0", 1, 6, "S"), ("s0", 1, 4), ("s0", 1, 5), ("s0", 1, 6), ("o0", 1, 7, "V"), ("s0", 1, 7),
+]
+
+
+def tile_bottleneck_transformer_pb_v_kernel(
+    tc, h_attn, x, conv3_w, bn3_g, bn3_b, bn3_m, bn3_v, sc_w, sc_b,
+    scbn_g, scbn_b, scbn_m, scbn_v, z, grad_out, out_0, out_1,
+):
+    nc = tc.nc
+    z_v = z.rearrange("b (g p j) n -> b g p j n", p=P, j=PACK)
+    g_v = grad_out.rearrange("b (g p j) n -> b g p j n", p=P, j=PACK)
+    w_v = sc_w.rearrange("(g p j) i -> g p j i", p=P, j=PACK)
+    x_v = x.rearrange("b (p t) n -> b p t n", t=IT)
+    o1_v = out_1.rearrange("(g m j) i -> g m j i", m=P, j=PACK)
+
+    with ExitStack() as ctx:
+        const = ctx.enter_context(tc.tile_pool(name="const", bufs=1))
+        keep = ctx.enter_context(tc.tile_pool(name="keep", bufs=1))
+        zpool = ctx.enter_context(tc.tile_pool(name="zpool", bufs=4))
+        gpool = ctx.enter_context(tc.tile_pool(name="gpool", bufs=4))
+        dzpool = ctx.enter_context(tc.tile_pool(name="dzpool", bufs=4))
+        ipool = ctx.enter_context(tc.tile_pool(name="ipool", bufs=2))
+        tgpool = ctx.enter_context(tc.tile_pool(name="tgpool", bufs=2))
+        wxpool = ctx.enter_context(tc.tile_pool(name="wxpool", bufs=3))
+        wipool = ctx.enter_context(tc.tile_pool(name="wipool", bufs=2))
+        st1pool = ctx.enter_context(tc.tile_pool(name="st1pool", bufs=3))
+        st0pool = ctx.enter_context(tc.tile_pool(name="st0pool", bufs=4))
+        tps = ctx.enter_context(tc.psum_pool(name="tps", bufs=2))
+        acc = ctx.enter_context(tc.psum_pool(name="acc", bufs=6))
+
+        cA = keep.tile([P, B, G, N], U32, name="cA", align_bytes=64)
+        sA = keep.tile([P, B, G, N], U8, name="sA", align_bytes=64)
+        cB = keep.tile([P, B, G, KP], U32, name="cB", align_bytes=64)
+        sB = keep.tile([P, B, G, KP], U8, name="sB", align_bytes=64)
+        cW = keep.tile([P, G, CIN], U32, name="cW", align_bytes=64)
+        sW = keep.tile([P, G, CIN], U8, name="sW", align_bytes=64)
+        cX = keep.tile([P, B, CIN], U32, name="cX", align_bytes=64)
+        sX = keep.tile([P, B, CIN], U8, name="sX", align_bytes=64)
+
+        ident = const.tile([P, P], F32, name="ident")
+        make_identity(nc, ident[:])
+
+        NV = G * PACK
+        g_bf = const.tile([P, NV], BF16, name="g_bf")
+        v_bf = const.tile([P, NV], BF16, name="v_bf")
+        v32 = const.tile([P, NV], F32, name="v32")
+        sd = const.tile([P, NV], F32, name="sd")
+        y0 = const.tile([P, NV], F32, name="y0")
+        t0 = const.tile([P, NV], F32, name="t0")
+        t1 = const.tile([P, NV], F32, name="t1")
+        t2 = const.tile([P, NV], F32, name="t2")
+        y1 = const.tile([P, NV], F32, name="y1")
+        a_col = const.tile([P, NV], F32, name="a_col")
+
+        T = {}
+
+        def copy_on(eng, out, in_):
+            if eng == "V":
+                nc.vector.tensor_copy(out=out, in_=in_)
+            else:
+                nc.scalar.copy(out=out, in_=in_)
+
+        def gv():
+            nc.sync.dma_start(out=v_bf[:].rearrange("p (g j) -> p g j", j=PACK), in_=scbn_v.rearrange("(g p j) -> p g j", p=P, j=PACK))
+            nc.sync.dma_start(out=g_bf[:].rearrange("p (g j) -> p g j", j=PACK), in_=scbn_g.rearrange("(g p j) -> p g j", p=P, j=PACK))
+
+        def a1():
+            nc.vector.tensor_scalar(out=v32[:], in0=v_bf[:], scalar1=EPS, scalar2=None, op0=ALU.add)
+
+        def sqrt():
+            nc.scalar.activation(out=sd[:], in_=v32[:], func=ACT.Sqrt)
+
+        def a2():
+            nc.vector.reciprocal(out=y0[:], in_=sd[:])
+            nc.vector.tensor_tensor(out=t0[:], in0=y0[:], in1=y0[:], op=ALU.mult)
+            nc.vector.tensor_tensor(out=t1[:], in0=t0[:], in1=v32[:], op=ALU.mult)
+            nc.vector.tensor_scalar(out=t2[:], in0=t1[:], scalar1=-0.5, scalar2=1.5, op0=ALU.mult, op1=ALU.add)
+            nc.vector.tensor_tensor(out=y1[:], in0=y0[:], in1=t2[:], op=ALU.mult)
+            nc.vector.tensor_tensor(out=a_col[:], in0=y1[:], in1=g_bf[:], op=ALU.mult)
+
+        def L(s):
+            g, b = ORDER[s]
+            T["z", s] = zpool.tile([P, PACK, N], F32, name="zt")
+            nc.sync.dma_start(out=T["z", s][:], in_=z_v[b, g])
+            T["g", s] = gpool.tile([P, PACK, N], BF16, name="gt")
+            nc.sync.dma_start(out=T["g", s][:], in_=g_v[b, g])
+
+        def Lh(s, h):
+            g, b = ORDER[s]
+            if h == 0:
+                T["z", s] = zpool.tile([P, PACK, N], F32, name="zt")
+                T["g", s] = gpool.tile([P, PACK, N], BF16, name="gt")
+            nc.sync.dma_start(out=T["z", s][:, 2 * h : 2 * h + 2, :], in_=z_v[b, g][:, 2 * h : 2 * h + 2, :])
+            nc.sync.dma_start(out=T["g", s][:, 2 * h : 2 * h + 2, :], in_=g_v[b, g][:, 2 * h : 2 * h + 2, :])
+
+        def maskh(s, h):
+            js = slice(2 * h, 2 * h + 2)
+            nc.vector.scalar_tensor_tensor(out=T["g", s][:, js, :], in0=T["z", s][:, js, :], scalar=0.0, in1=T["g", s][:, js, :], op0=ALU.is_gt, op1=ALU.mult)
+
+        def LX(b):
+            T["x", b] = wxpool.tile([P, IT * N], BF16, name="wx")
+            nc.sync.dma_start(out=T["x", b][:].rearrange("p (t n) -> p t n", t=IT), in_=x_v[b])
+
+        def LW(g):
+            T["w", g] = wxpool.tile([P, PACK * CIN], BF16, name="wx")
+            nc.sync.dma_start(out=T["w", g][:].rearrange("p (j i) -> p j i", j=PACK), in_=w_v[g])
+
+        def mask(s):
+            nc.vector.scalar_tensor_tensor(out=T["g", s][:], in0=T["z", s][:], scalar=0.0, in1=T["g", s][:], op0=ALU.is_gt, op1=ALU.mult)
+
+        def scale(s):
+            g, b = ORDER[s]
+            T["dz", s] = dzpool.tile([P, PACK, N], BF16, name="dz")
+            for j in range(PACK):
+                nc.vector.tensor_scalar(out=T["dz", s][:, j, :], in0=T["g", s][:, j, :], scalar1=a_col[:, PACK * g + j : PACK * g + j + 1], scalar2=None, op0=ALU.mult)
+
+        def weave(s, eng="V"):
+            T["dzi", s] = ipool.tile([P, N, PACK], BF16, name="dzi", align_bytes=64)
+            copy_on(eng, T["dzi", s][:], T["dz", s][:].rearrange("p j n -> p n j"))
+
+        def qa(s):
+            g, b = ORDER[s]
+            nc.vector.quantize_mx(out=cA[:, b, g, :].bitcast(E5), scales=sA[:, b, g, :], in_=T["dzi", s][:].rearrange("p n j -> p (n j)"))
+
+        def turn(s):
+            words = T["dz", s][:].rearrange("p j n -> p (j n)").bitcast(F32)
+            for h in range(2):
+                T["ptd", s, h] = tps.tile([P, 2, 2, P], F32, name="pt")
+                for a in range(2):
+                    for u in range(2):
+                        j = 2 * h + a
+                        nc.tensor.transpose(T["ptd", s, h][:, a, u, :], words[:, 256 * j + u : 256 * (j + 1) : 2], ident[:])
+
+        def unturn(s, eng="S"):
+            T["dzt", s] = tgpool.tile([P, KP * PACK], BF16, name="dzt", align_bytes=64)
+            dzt_w = T["dzt", s][:].bitcast(F32).rearrange("p (j m u) -> p j m u", j=PACK, u=2)
+            for h in range(2):
+                copy_on(eng, dzt_w[:, 2 * h : 2 * h + 2, :, :], T["ptd", s, h][:].rearrange("p a u m -> p a m u"))
+
+        def qb(s):
+            g, b = ORDER[s]
+            nc.vector.quantize_mx(out=cB[:, b, g, :].bitcast(E5), scales=sB[:, b, g, :], in_=T["dzt", s][:])
+
+        def xt(b, h):
+            words = T["x", b][:].bitcast(F32)
+            T["ptx", b, h] = tps.tile([P, 2, 2, P], F32, name="pt")
+            for a in range(2):
+                for u in range(2):
+                    t = 2 * h + a
+                    nc.tensor.transpose(T["ptx", b, h][:, a, u, :], words[:, 256 * t + u : 256 * (t + 1) : 2], ident[:])
+
+        def xc(b, h, eng="S"):
+            if h == 0:
+                T["xg", b] = wipool.tile([P, CIN * PACK], BF16, name="wi", align_bytes=64)
+            xg_w = T["xg", b][:].bitcast(F32).rearrange("p (m t u) -> p m t u", t=IT, u=2)
+            copy_on(eng, xg_w[:, :, 2 * h : 2 * h + 2, :], T["ptx", b, h][:].rearrange("p a u m -> p m a u"))
+
+        def xq(b):
+            nc.vector.quantize_mx(out=cX[:, b, :].bitcast(E4), scales=sX[:, b, :], in_=T["xg", b][:])
+
+        def wi(g, h, eng):
+            if h == 0:
+                T["wi", g] = wipool.tile([P, CIN * PACK], BF16, name="wi", align_bytes=64)
+            dst = T["wi", g][:].rearrange("p (i j) -> p i j", j=PACK)
+            src = T["w", g][:].rearrange("p (j i) -> p i j", j=PACK)
+            copy_on(eng, dst[:, 256 * h : 256 * (h + 1), :], src[:, 256 * h : 256 * (h + 1), :])
+
+        def wq(g):
+            nc.vector.quantize_mx(out=cW[:, g, :].bitcast(E4), scales=sW[:, g, :], in_=T["wi", g][:])
+
+        def m1(g, q):
+            j, ih = q // 2, q % 2
+            T["p1", g, q] = acc.tile([P, N], F32, name="ps")
+            for b in range(B):
+                nc.tensor.matmul_mx(
+                    out=T["p1", g, q][:],
+                    lhsT=cB[:, b, g, P * j : P * (j + 1)].bitcast(E5), lhsT_scale=sB[:, b, g, P * j : P * (j + 1)],
+                    rhs=cX[:, b, N * ih : N * (ih + 1)].bitcast(E4), rhs_scale=sX[:, b, N * ih : N * (ih + 1)],
+                    start=(b == 0), stop=(b == B - 1),
+                )
+
+        def o1(g, q, eng="S"):
+            if q % 4 == 0:
+                T["sa", g, q // 4] = st1pool.tile([P, 2, CIN], F32, name="sa")
+            j, ih = q // 2, q % 2
+            copy_on(eng, T["sa", g, q // 4][:, j % 2, N * ih : N * (ih + 1)], T["p1", g, q][:])
+
+        def s1(g, h):
+            nc.sync.dma_start(out=o1_v[g][:, 2 * h : 2 * h + 2, :], in_=T["sa", g, h][:])
+
+        def m0(b, t, gs):
+            if gs[0] == 0:
+                T["p0", b, t] = acc.tile([P, N], F32, name="ps")
+            for g in gs:
+                nc.tensor.matmul_mx(
+                    out=T["p0", b, t][:],
+                    lhsT=cW[:, g, P * t : P * (t + 1)].bitcast(E4), lhsT_scale=sW[:, g, P * t : P * (t + 1)],
+                    rhs=cA[:, b, g, :].bitcast(E5), rhs_scale=sA[:, b, g, :],
+                    start=(g == 0), stop=(g == G - 1),
+                )
+
+        def o0(b, t, eng="S"):
+            T["sb", b, t] = st0pool.tile([P, N], F32, name="sb")
+            copy_on(eng, T["sb", b, t][:], T["p0", b, t][:])
+
+        def s0(b, t):
+            nc.sync.dma_start(out=out_0[b, P * t : P * (t + 1), :], in_=T["sb", b, t][:])
+
+        FN = {"gv": gv, "a1": a1, "sqrt": sqrt, "a2": a2, "L": L, "Lh": Lh, "maskh": maskh, "LX": LX, "LW": LW, "mask": mask, "scale": scale, "weave": weave,
+              "qa": qa, "turn": turn, "unturn": unturn, "qb": qb, "xt": xt, "xc": xc, "xq": xq, "wi": wi, "wq": wq,
+              "m1": m1, "o1": o1, "s1": s1, "m0": m0, "o0": o0, "s0": s0}
+        with tc.manual_schedule():
+            for step in RUN:
+                FN[step[0]](*step[1:])

@@ -10,8 +10,8 @@ F32 = mybir.dt.float32
 BF16 = mybir.dt.bfloat16
 U32 = mybir.dt.uint32
 U8 = mybir.dt.uint8
-E4 = mybir.dt.float8_e4m3fn_x4
-E5 = mybir.dt.float8_e5m2_x4
+E4M3 = mybir.dt.float8_e4m3fn_x4
+E5M2 = mybir.dt.float8_e5m2_x4
 ALU = mybir.AluOpType
 ACT = mybir.ActivationFunctionType
 
@@ -20,56 +20,13 @@ PACK = 4
 KP = P * PACK
 G = COUT // KP
 IT = CIN // P
+WORDS = N // 2
+QUARTER = CIN // 4
+
+OPEN_TILES = 5
 
 FLOPS = 2 * 2 * COUT * CIN * B * N
 BYTES = 2 * (B * CIN * N + COUT * CIN + B * COUT * N + 2 * COUT) + 4 * (B * COUT * N + B * CIN * N + COUT * CIN)
-
-ORDER = [(0, 0), (1, 0), (2, 0), (3, 0), (0, 1), (1, 1), (2, 1), (3, 1)]
-
-RUN = [
-    ("gv",), ("Lh", 0, 0), ("Lh", 0, 1), ("LW", 0), ("L", 1), ("LW", 1),
-    ("L", 2), ("LW", 2), ("L", 3), ("a1",), ("sqrt",), ("a2",),
-    ("maskh", 0, 0), ("maskh", 0, 1), ("scale", 0), ("weave", 0), ("turn", 0), ("wi", 0, 0, "S"),
-    ("unturn", 0), ("wi", 0, 1, "S"), ("mask", 1), ("wi", 0, 2, "S"), ("wi", 0, 3, "S"), ("wi", 1, 0, "S"),
-    ("LW", 3), ("wq", 0), ("wi", 1, 1, "S"), ("qb", 0), ("scale", 1), ("wi", 1, 2, "S"),
-    ("qa", 0), ("turn", 1), ("weave", 1), ("wi", 1, 3, "S"), ("m0", 0, 0, (0,)), ("m0", 0, 1, (0,)),
-    ("m0", 0, 2, (0,)), ("unturn", 1), ("mask", 2), ("LX", 0), ("L", 4), ("m0", 0, 3, (0,)),
-    ("m0", 0, 4, (0,)), ("m0", 0, 5, (0,)), ("wi", 2, 0, "S"), ("wq", 1), ("wi", 2, 1, "S"), ("qb", 1),
-    ("wi", 2, 2, "S"), ("scale", 2), ("wi", 2, 3, "S"), ("qa", 1), ("turn", 2), ("weave", 2),
-    ("unturn", 2), ("LX", 1), ("L", 5), ("m0", 0, 0, (1,)), ("L", 6), ("m0", 0, 1, (1,)),
-    ("mask", 3), ("m0", 0, 2, (1,)), ("wi", 3, 0, "S"), ("m0", 0, 3, (1,)), ("m0", 0, 4, (1,)), ("m0", 0, 5, (1,)),
-    ("wi", 3, 1, "S"), ("xt", 0, 0), ("wq", 2), ("L", 7), ("wi", 3, 2, "S"), ("xt", 0, 1),
-    ("qb", 2), ("xc", 0, 0), ("scale", 3), ("xc", 0, 1), ("xt", 0, 2), ("wi", 3, 3, "S"),
-    ("qa", 2), ("xt", 0, 3), ("weave", 3), ("xc", 0, 2), ("xc", 0, 3), ("turn", 3),
-    ("xq", 0), ("unturn", 3), ("m0", 0, 0, (2,)), ("m0", 0, 1, (2,)), ("mask", 4), ("m0", 0, 2, (2,)),
-    ("m0", 0, 3, (2,)), ("m0", 0, 4, (2,)), ("m0", 0, 5, (2,)), ("xt", 1, 0), ("xt", 1, 1), ("wq", 3),
-    ("qb", 3), ("xc", 1, 0), ("scale", 4), ("xc", 1, 1), ("xt", 1, 2), ("xt", 1, 3),
-    ("qa", 3), ("xc", 1, 2), ("xc", 1, 3), ("turn", 4), ("xq", 1), ("unturn", 4),
-    ("m0", 0, 0, (3,)), ("m0", 0, 1, (3,)), ("mask", 5), ("m0", 0, 2, (3,)), ("o0", 0, 0, "S"), ("m0", 0, 3, (3,)),
-    ("m0", 0, 4, (3,)), ("o0", 0, 1, "S"), ("s0", 0, 0), ("m0", 0, 5, (3,)), ("m0", 0, 6, (0,1,2,3)), ("o0", 0, 2, "S"),
-    ("s0", 0, 1), ("o0", 0, 3, "S"), ("s0", 0, 2), ("scale", 5), ("m0", 0, 7, (0,1,2,3)), ("s0", 0, 3),
-    ("qb", 4), ("turn", 5), ("o0", 0, 4, "S"), ("mask", 6), ("o0", 0, 5, "S"), ("s0", 0, 4),
-    ("m1", 0, 0), ("unturn", 5), ("s0", 0, 5), ("m1", 0, 1), ("o0", 0, 6, "S"), ("m1", 0, 2),
-    ("scale", 6), ("o0", 0, 7, "S"), ("m1", 0, 3), ("s0", 0, 6), ("qb", 5), ("o1", 0, 0, "S"),
-    ("turn", 6), ("s0", 0, 7), ("weave", 4), ("o1", 0, 1, "S"), ("unturn", 6), ("m1", 0, 4),
-    ("mask", 7), ("m1", 0, 5), ("o1", 0, 2, "S"), ("m1", 0, 6), ("o1", 0, 3, "S"), ("m1", 0, 7),
-    ("o1", 0, 4, "S"), ("s1", 0, 0), ("m1", 1, 0), ("qa", 4), ("o1", 0, 5, "S"), ("m1", 1, 1),
-    ("o1", 0, 6, "S"), ("scale", 7), ("m1", 1, 2), ("o1", 0, 7, "S"), ("m1", 1, 3), ("qb", 6),
-    ("o1", 1, 0, "S"), ("s1", 0, 1), ("turn", 7), ("weave", 5), ("o1", 1, 1, "S"), ("unturn", 7),
-    ("m1", 1, 4), ("qa", 5), ("m1", 1, 5), ("o1", 1, 2, "S"), ("qb", 7), ("m1", 1, 6),
-    ("o1", 1, 3, "S"), ("weave", 6), ("m1", 1, 7), ("o1", 1, 4, "S"), ("s1", 1, 0), ("m1", 2, 0),
-    ("o1", 1, 5, "S"), ("m1", 2, 1), ("qa", 6), ("o1", 1, 6, "S"), ("m1", 2, 2), ("weave", 7),
-    ("o1", 1, 7, "S"), ("m1", 2, 3), ("o1", 2, 0, "S"), ("s1", 1, 1), ("m1", 2, 4), ("o1", 2, 1, "S"),
-    ("qa", 7), ("m1", 2, 5), ("o1", 2, 2, "S"), ("m1", 2, 6), ("o1", 2, 3, "S"), ("m1", 2, 7),
-    ("s1", 2, 0), ("o1", 2, 4, "S"), ("m1", 3, 0), ("o1", 2, 5, "S"), ("m1", 3, 1), ("o1", 2, 6, "S"),
-    ("m1", 3, 2), ("o1", 2, 7, "S"), ("m1", 3, 3), ("o1", 3, 0, "S"), ("s1", 2, 1), ("m1", 3, 4),
-    ("o1", 3, 1, "S"), ("m1", 3, 5), ("o1", 3, 2, "S"), ("m1", 3, 6), ("o1", 3, 3, "S"), ("m1", 3, 7),
-    ("o1", 3, 4, "S"), ("s1", 3, 0), ("m0", 1, 0, (0,1,2,3)), ("o1", 3, 5, "S"), ("o1", 3, 6, "S"), ("m0", 1, 1, (0,1,2,3)),
-    ("o1", 3, 7, "S"), ("o0", 1, 0, "S"), ("s1", 3, 1), ("m0", 1, 2, (0,1,2,3)), ("o0", 1, 1, "V"), ("s0", 1, 0),
-    ("s0", 1, 1), ("m0", 1, 3, (0,1,2,3)), ("o0", 1, 2, "S"), ("s0", 1, 2), ("m0", 1, 4, (0,1,2,3)), ("o0", 1, 3, "V"),
-    ("s0", 1, 3), ("m0", 1, 5, (0,1,2,3)), ("m0", 1, 6, (0,1,2,3)), ("o0", 1, 5, "V"), ("o0", 1, 4, "S"), ("m0", 1, 7, (0,1,2,3)),
-    ("o0", 1, 6, "S"), ("s0", 1, 4), ("s0", 1, 5), ("s0", 1, 6), ("o0", 1, 7, "V"), ("s0", 1, 7),
-]
 
 
 def tile_bottleneck_transformer_pb_v_kernel(
@@ -77,208 +34,299 @@ def tile_bottleneck_transformer_pb_v_kernel(
     scbn_g, scbn_b, scbn_m, scbn_v, z, grad_out, out_0, out_1,
 ):
     nc = tc.nc
-    z_v = z.rearrange("b (g p j) n -> b g p j n", p=P, j=PACK)
-    g_v = grad_out.rearrange("b (g p j) n -> b g p j n", p=P, j=PACK)
-    w_v = sc_w.rearrange("(g p j) i -> g p j i", p=P, j=PACK)
-    x_v = x.rearrange("b (p t) n -> b p t n", t=IT)
-    o1_v = out_1.rearrange("(g m j) i -> g m j i", m=P, j=PACK)
+
+    z_view = z.rearrange("b (g p j) n -> b g p j n", p=P, j=PACK)
+    grad_view = grad_out.rearrange("b (g p j) n -> b g p j n", p=P, j=PACK)
+    w_view = sc_w.rearrange("(g p j) i -> g p j i", p=P, j=PACK)
+    x_view = x.rearrange("b (p t) n -> b p t n", t=IT)
+    dw_view = out_1.rearrange("(g m j) i -> g m j i", m=P, j=PACK)
 
     with ExitStack() as ctx:
         const = ctx.enter_context(tc.tile_pool(name="const", bufs=1))
         keep = ctx.enter_context(tc.tile_pool(name="keep", bufs=1))
-        zpool = ctx.enter_context(tc.tile_pool(name="zpool", bufs=4))
-        gpool = ctx.enter_context(tc.tile_pool(name="gpool", bufs=4))
-        dzpool = ctx.enter_context(tc.tile_pool(name="dzpool", bufs=4))
-        ipool = ctx.enter_context(tc.tile_pool(name="ipool", bufs=2))
-        tgpool = ctx.enter_context(tc.tile_pool(name="tgpool", bufs=2))
-        wxpool = ctx.enter_context(tc.tile_pool(name="wxpool", bufs=3))
-        wipool = ctx.enter_context(tc.tile_pool(name="wipool", bufs=2))
-        st1pool = ctx.enter_context(tc.tile_pool(name="st1pool", bufs=3))
-        st0pool = ctx.enter_context(tc.tile_pool(name="st0pool", bufs=4))
-        tps = ctx.enter_context(tc.psum_pool(name="tps", bufs=2))
-        acc = ctx.enter_context(tc.psum_pool(name="acc", bufs=6))
+        z_pool = ctx.enter_context(tc.tile_pool(name="z_pool", bufs=4))
+        grad_pool = ctx.enter_context(tc.tile_pool(name="grad_pool", bufs=4))
+        dz_pool = ctx.enter_context(tc.tile_pool(name="dz_pool", bufs=4))
+        by_channel_pool = ctx.enter_context(tc.tile_pool(name="by_channel_pool", bufs=2))
+        by_token_pool = ctx.enter_context(tc.tile_pool(name="by_token_pool", bufs=2))
+        grouped_pool = ctx.enter_context(tc.tile_pool(name="grouped_pool", bufs=2))
+        raw_pool = ctx.enter_context(tc.tile_pool(name="raw_pool", bufs=3))
+        dw_pool = ctx.enter_context(tc.tile_pool(name="dw_pool", bufs=3))
+        dx_pool = ctx.enter_context(tc.tile_pool(name="dx_pool", bufs=8))
+        turn_psum = ctx.enter_context(tc.psum_pool(name="turn_psum", bufs=8 - OPEN_TILES))
+        acc_psum = ctx.enter_context(tc.psum_pool(name="acc_psum", bufs=OPEN_TILES))
 
-        cA = keep.tile([P, B, G, N], U32, name="cA", align_bytes=64)
-        sA = keep.tile([P, B, G, N], U8, name="sA", align_bytes=64)
-        cB = keep.tile([P, B, G, KP], U32, name="cB", align_bytes=64)
-        sB = keep.tile([P, B, G, KP], U8, name="sB", align_bytes=64)
-        cW = keep.tile([P, G, CIN], U32, name="cW", align_bytes=64)
-        sW = keep.tile([P, G, CIN], U8, name="sW", align_bytes=64)
-        cX = keep.tile([P, B, CIN], U32, name="cX", align_bytes=64)
-        sX = keep.tile([P, B, CIN], U8, name="sX", align_bytes=64)
+        dzc_codes = keep.tile([P, B, G, N], U32, name="dzc_codes", align_bytes=64)
+        dzc_scales = keep.tile([P, B, G, N], U8, name="dzc_scales", align_bytes=64)
+        dzt_codes = keep.tile([P, B, G, KP], U32, name="dzt_codes", align_bytes=64)
+        dzt_scales = keep.tile([P, B, G, KP], U8, name="dzt_scales", align_bytes=64)
+        w_codes = keep.tile([P, G, CIN], U32, name="w_codes", align_bytes=64)
+        w_scales = keep.tile([P, G, CIN], U8, name="w_scales", align_bytes=64)
+        x_codes = keep.tile([P, B, CIN], U32, name="x_codes", align_bytes=64)
+        x_scales = keep.tile([P, B, CIN], U8, name="x_scales", align_bytes=64)
 
         ident = const.tile([P, P], F32, name="ident")
         make_identity(nc, ident[:])
 
-        NV = G * PACK
-        g_bf = const.tile([P, NV], BF16, name="g_bf")
-        v_bf = const.tile([P, NV], BF16, name="v_bf")
-        v32 = const.tile([P, NV], F32, name="v32")
-        sd = const.tile([P, NV], F32, name="sd")
-        y0 = const.tile([P, NV], F32, name="y0")
-        t0 = const.tile([P, NV], F32, name="t0")
-        t1 = const.tile([P, NV], F32, name="t1")
-        t2 = const.tile([P, NV], F32, name="t2")
-        y1 = const.tile([P, NV], F32, name="y1")
-        a_col = const.tile([P, NV], F32, name="a_col")
+        gain_bf = const.tile([P, G * PACK], BF16, name="gain_bf")
+        var_bf = const.tile([P, G * PACK], BF16, name="var_bf")
+        var_eps = const.tile([P, G * PACK], F32, name="var_eps")
+        std = const.tile([P, G * PACK], F32, name="std")
+        rstd = const.tile([P, G * PACK], F32, name="rstd")
+        newton_a = const.tile([P, G * PACK], F32, name="newton_a")
+        newton_b = const.tile([P, G * PACK], F32, name="newton_b")
+        newton_c = const.tile([P, G * PACK], F32, name="newton_c")
+        rstd_fine = const.tile([P, G * PACK], F32, name="rstd_fine")
+        slope = const.tile([P, G * PACK], F32, name="slope")
 
-        T = {}
+        z_tile, grad_tile, dz_tile, by_channel, by_token = {}, {}, {}, {}, {}
+        raw_w, raw_x, grouped_w, grouped_x = {}, {}, {}, {}
+        turned, dx_acc, dw_acc, dw_rows = {}, {}, {}, {}
 
-        def copy_on(eng, out, in_):
-            if eng == "V":
+        def copy_on(engine, out, in_):
+            if engine == "vector":
                 nc.vector.tensor_copy(out=out, in_=in_)
             else:
                 nc.scalar.copy(out=out, in_=in_)
 
-        def gv():
-            nc.sync.dma_start(out=v_bf[:].rearrange("p (g j) -> p g j", j=PACK), in_=scbn_v.rearrange("(g p j) -> p g j", p=P, j=PACK))
-            nc.sync.dma_start(out=g_bf[:].rearrange("p (g j) -> p g j", j=PACK), in_=scbn_g.rearrange("(g p j) -> p g j", p=P, j=PACK))
+        def load_slope_inputs():
+            nc.scalar.dma_start(out=var_bf[:].rearrange("p (g j) -> p g j", j=PACK), in_=scbn_v.rearrange("(g p j) -> p g j", p=P, j=PACK))
+            nc.scalar.dma_start(out=gain_bf[:].rearrange("p (g j) -> p g j", j=PACK), in_=scbn_g.rearrange("(g p j) -> p g j", p=P, j=PACK))
 
-        def a1():
-            nc.vector.tensor_scalar(out=v32[:], in0=v_bf[:], scalar1=EPS, scalar2=None, op0=ALU.add)
+        def load_chunk(s, pieces=1):
+            b, g = divmod(s, G)
+            z_tile[s] = z_pool.tile([P, PACK, N], F32, name="z_tile")
+            grad_tile[s] = grad_pool.tile([P, PACK, N], BF16, name="grad_tile")
+            step = PACK // pieces
+            for j0 in range(0, PACK, step):
+                nc.sync.dma_start(out=z_tile[s][:, j0 : j0 + step, :], in_=z_view[b, g][:, j0 : j0 + step, :])
+                nc.sync.dma_start(out=grad_tile[s][:, j0 : j0 + step, :], in_=grad_view[b, g][:, j0 : j0 + step, :])
 
-        def sqrt():
-            nc.scalar.activation(out=sd[:], in_=v32[:], func=ACT.Sqrt)
+        def load_w(g):
+            raw_w[g] = raw_pool.tile([P, PACK, CIN], BF16, name="raw")
+            nc.sync.dma_start(out=raw_w[g][:], in_=w_view[g])
 
-        def a2():
-            nc.vector.reciprocal(out=y0[:], in_=sd[:])
-            nc.vector.tensor_tensor(out=t0[:], in0=y0[:], in1=y0[:], op=ALU.mult)
-            nc.vector.tensor_tensor(out=t1[:], in0=t0[:], in1=v32[:], op=ALU.mult)
-            nc.vector.tensor_scalar(out=t2[:], in0=t1[:], scalar1=-0.5, scalar2=1.5, op0=ALU.mult, op1=ALU.add)
-            nc.vector.tensor_tensor(out=y1[:], in0=y0[:], in1=t2[:], op=ALU.mult)
-            nc.vector.tensor_tensor(out=a_col[:], in0=y1[:], in1=g_bf[:], op=ALU.mult)
+        def load_x(b):
+            raw_x[b] = raw_pool.tile([P, IT * N], BF16, name="raw")
+            nc.sync.dma_start(out=raw_x[b][:].rearrange("p (t n) -> p t n", t=IT), in_=x_view[b])
 
-        def L(s):
-            g, b = ORDER[s]
-            T["z", s] = zpool.tile([P, PACK, N], F32, name="zt")
-            nc.sync.dma_start(out=T["z", s][:], in_=z_v[b, g])
-            T["g", s] = gpool.tile([P, PACK, N], BF16, name="gt")
-            nc.sync.dma_start(out=T["g", s][:], in_=g_v[b, g])
+        def slope_variance():
+            nc.vector.tensor_scalar(out=var_eps[:], in0=var_bf[:], scalar1=EPS, scalar2=None, op0=ALU.add)
 
-        def Lh(s, h):
-            g, b = ORDER[s]
-            if h == 0:
-                T["z", s] = zpool.tile([P, PACK, N], F32, name="zt")
-                T["g", s] = gpool.tile([P, PACK, N], BF16, name="gt")
-            nc.sync.dma_start(out=T["z", s][:, 2 * h : 2 * h + 2, :], in_=z_v[b, g][:, 2 * h : 2 * h + 2, :])
-            nc.sync.dma_start(out=T["g", s][:, 2 * h : 2 * h + 2, :], in_=g_v[b, g][:, 2 * h : 2 * h + 2, :])
+        def slope_sqrt():
+            nc.scalar.activation(out=std[:], in_=var_eps[:], func=ACT.Sqrt)
 
-        def maskh(s, h):
-            js = slice(2 * h, 2 * h + 2)
-            nc.vector.scalar_tensor_tensor(out=T["g", s][:, js, :], in0=T["z", s][:, js, :], scalar=0.0, in1=T["g", s][:, js, :], op0=ALU.is_gt, op1=ALU.mult)
+        def slope_finish():
+            nc.vector.reciprocal(out=rstd[:], in_=std[:])
+            nc.vector.tensor_tensor(out=newton_a[:], in0=rstd[:], in1=rstd[:], op=ALU.mult)
+            nc.vector.tensor_tensor(out=newton_b[:], in0=newton_a[:], in1=var_eps[:], op=ALU.mult)
+            nc.vector.tensor_scalar(out=newton_c[:], in0=newton_b[:], scalar1=-0.5, scalar2=1.5, op0=ALU.mult, op1=ALU.add)
+            nc.vector.tensor_tensor(out=rstd_fine[:], in0=rstd[:], in1=newton_c[:], op=ALU.mult)
+            nc.vector.tensor_tensor(out=slope[:], in0=rstd_fine[:], in1=gain_bf[:], op=ALU.mult)
 
-        def LX(b):
-            T["x", b] = wxpool.tile([P, IT * N], BF16, name="wx")
-            nc.sync.dma_start(out=T["x", b][:].rearrange("p (t n) -> p t n", t=IT), in_=x_v[b])
-
-        def LW(g):
-            T["w", g] = wxpool.tile([P, PACK * CIN], BF16, name="wx")
-            nc.sync.dma_start(out=T["w", g][:].rearrange("p (j i) -> p j i", j=PACK), in_=w_v[g])
-
-        def mask(s):
-            nc.vector.scalar_tensor_tensor(out=T["g", s][:], in0=T["z", s][:], scalar=0.0, in1=T["g", s][:], op0=ALU.is_gt, op1=ALU.mult)
+        def mask(s, js=slice(0, PACK)):
+            nc.vector.scalar_tensor_tensor(
+                out=grad_tile[s][:, js, :], in0=z_tile[s][:, js, :], scalar=0.0, in1=grad_tile[s][:, js, :],
+                op0=ALU.is_gt, op1=ALU.mult,
+            )
 
         def scale(s):
-            g, b = ORDER[s]
-            T["dz", s] = dzpool.tile([P, PACK, N], BF16, name="dz")
+            g = s % G
+            dz_tile[s] = dz_pool.tile([P, PACK, N], BF16, name="dz_tile")
             for j in range(PACK):
-                nc.vector.tensor_scalar(out=T["dz", s][:, j, :], in0=T["g", s][:, j, :], scalar1=a_col[:, PACK * g + j : PACK * g + j + 1], scalar2=None, op0=ALU.mult)
-
-        def weave(s, eng="V"):
-            T["dzi", s] = ipool.tile([P, N, PACK], BF16, name="dzi", align_bytes=64)
-            copy_on(eng, T["dzi", s][:], T["dz", s][:].rearrange("p j n -> p n j"))
-
-        def qa(s):
-            g, b = ORDER[s]
-            nc.vector.quantize_mx(out=cA[:, b, g, :].bitcast(E5), scales=sA[:, b, g, :], in_=T["dzi", s][:].rearrange("p n j -> p (n j)"))
-
-        def turn(s):
-            words = T["dz", s][:].rearrange("p j n -> p (j n)").bitcast(F32)
-            for h in range(2):
-                T["ptd", s, h] = tps.tile([P, 2, 2, P], F32, name="pt")
-                for a in range(2):
-                    for u in range(2):
-                        j = 2 * h + a
-                        nc.tensor.transpose(T["ptd", s, h][:, a, u, :], words[:, 256 * j + u : 256 * (j + 1) : 2], ident[:])
-
-        def unturn(s, eng="S"):
-            T["dzt", s] = tgpool.tile([P, KP * PACK], BF16, name="dzt", align_bytes=64)
-            dzt_w = T["dzt", s][:].bitcast(F32).rearrange("p (j m u) -> p j m u", j=PACK, u=2)
-            for h in range(2):
-                copy_on(eng, dzt_w[:, 2 * h : 2 * h + 2, :, :], T["ptd", s, h][:].rearrange("p a u m -> p a m u"))
-
-        def qb(s):
-            g, b = ORDER[s]
-            nc.vector.quantize_mx(out=cB[:, b, g, :].bitcast(E5), scales=sB[:, b, g, :], in_=T["dzt", s][:])
-
-        def xt(b, h):
-            words = T["x", b][:].bitcast(F32)
-            T["ptx", b, h] = tps.tile([P, 2, 2, P], F32, name="pt")
-            for a in range(2):
-                for u in range(2):
-                    t = 2 * h + a
-                    nc.tensor.transpose(T["ptx", b, h][:, a, u, :], words[:, 256 * t + u : 256 * (t + 1) : 2], ident[:])
-
-        def xc(b, h, eng="S"):
-            if h == 0:
-                T["xg", b] = wipool.tile([P, CIN * PACK], BF16, name="wi", align_bytes=64)
-            xg_w = T["xg", b][:].bitcast(F32).rearrange("p (m t u) -> p m t u", t=IT, u=2)
-            copy_on(eng, xg_w[:, :, 2 * h : 2 * h + 2, :], T["ptx", b, h][:].rearrange("p a u m -> p m a u"))
-
-        def xq(b):
-            nc.vector.quantize_mx(out=cX[:, b, :].bitcast(E4), scales=sX[:, b, :], in_=T["xg", b][:])
-
-        def wi(g, h, eng):
-            if h == 0:
-                T["wi", g] = wipool.tile([P, CIN * PACK], BF16, name="wi", align_bytes=64)
-            dst = T["wi", g][:].rearrange("p (i j) -> p i j", j=PACK)
-            src = T["w", g][:].rearrange("p (j i) -> p i j", j=PACK)
-            copy_on(eng, dst[:, 256 * h : 256 * (h + 1), :], src[:, 256 * h : 256 * (h + 1), :])
-
-        def wq(g):
-            nc.vector.quantize_mx(out=cW[:, g, :].bitcast(E4), scales=sW[:, g, :], in_=T["wi", g][:])
-
-        def m1(g, q):
-            j, ih = q // 2, q % 2
-            T["p1", g, q] = acc.tile([P, N], F32, name="ps")
-            for b in range(B):
-                nc.tensor.matmul_mx(
-                    out=T["p1", g, q][:],
-                    lhsT=cB[:, b, g, P * j : P * (j + 1)].bitcast(E5), lhsT_scale=sB[:, b, g, P * j : P * (j + 1)],
-                    rhs=cX[:, b, N * ih : N * (ih + 1)].bitcast(E4), rhs_scale=sX[:, b, N * ih : N * (ih + 1)],
-                    start=(b == 0), stop=(b == B - 1),
+                nc.vector.tensor_scalar(
+                    out=dz_tile[s][:, j, :], in0=grad_tile[s][:, j, :],
+                    scalar1=slope[:, PACK * g + j : PACK * g + j + 1], scalar2=None, op0=ALU.mult,
                 )
 
-        def o1(g, q, eng="S"):
-            if q % 4 == 0:
-                T["sa", g, q // 4] = st1pool.tile([P, 2, CIN], F32, name="sa")
-            j, ih = q // 2, q % 2
-            copy_on(eng, T["sa", g, q // 4][:, j % 2, N * ih : N * (ih + 1)], T["p1", g, q][:])
+        def weave(s):
+            by_channel[s] = by_channel_pool.tile([P, N, PACK], BF16, name="by_channel", align_bytes=64)
+            nc.vector.tensor_copy(out=by_channel[s][:], in_=dz_tile[s][:].rearrange("p j n -> p n j"))
 
-        def s1(g, h):
-            nc.sync.dma_start(out=o1_v[g][:, 2 * h : 2 * h + 2, :], in_=T["sa", g, h][:])
+        def quantize_by_channel(s):
+            b, g = divmod(s, G)
+            nc.vector.quantize_mx(
+                out=dzc_codes[:, b, g, :].bitcast(E5M2), scales=dzc_scales[:, b, g, :],
+                in_=by_channel[s][:].rearrange("p n j -> p (n j)"),
+            )
 
-        def m0(b, t, gs):
-            if gs[0] == 0:
-                T["p0", b, t] = acc.tile([P, N], F32, name="ps")
-            for g in gs:
+        def turn(s):
+            words = dz_tile[s][:].rearrange("p j n -> p (j n)").bitcast(F32)
+            for h in range(2):
+                turned[s, h] = turn_psum.tile([P, 2, 2, P], F32, name="turned")
+                for a in range(2):
+                    for u in range(2):
+                        row = 2 * h + a
+                        nc.tensor.transpose(turned[s, h][:, a, u, :], words[:, WORDS * row + u : WORDS * (row + 1) : 2], ident[:])
+
+        def unturn(s):
+            by_token[s] = by_token_pool.tile([P, KP * PACK], BF16, name="by_token", align_bytes=64)
+            dst = by_token[s][:].bitcast(F32).rearrange("p (j m u) -> p j m u", j=PACK, u=2)
+            for h in range(2):
+                nc.scalar.copy(out=dst[:, 2 * h : 2 * h + 2, :, :], in_=turned[s, h][:].rearrange("p a u m -> p a m u"))
+
+        def quantize_by_token(s):
+            b, g = divmod(s, G)
+            nc.vector.quantize_mx(out=dzt_codes[:, b, g, :].bitcast(E5M2), scales=dzt_scales[:, b, g, :], in_=by_token[s][:])
+
+        def turn_x(b):
+            words = raw_x[b][:].bitcast(F32)
+            grouped_x[b] = grouped_pool.tile([P, CIN * PACK], BF16, name="grouped", align_bytes=64)
+            dst = grouped_x[b][:].bitcast(F32).rearrange("p (m t u) -> p m t u", t=IT, u=2)
+            for h in range(IT // 2):
+                turned_x = turn_psum.tile([P, 2, 2, P], F32, name="turned")
+                for a in range(2):
+                    for u in range(2):
+                        row = 2 * h + a
+                        nc.tensor.transpose(turned_x[:, a, u, :], words[:, WORDS * row + u : WORDS * (row + 1) : 2], ident[:])
+                nc.scalar.copy(out=dst[:, :, 2 * h : 2 * h + 2, :], in_=turned_x[:].rearrange("p a u m -> p m a u"))
+
+        def quantize_x(b):
+            nc.vector.quantize_mx(out=x_codes[:, b, :].bitcast(E4M3), scales=x_scales[:, b, :], in_=grouped_x[b][:])
+
+        def weave_w(g, quarters):
+            if quarters[0] == 0:
+                grouped_w[g] = grouped_pool.tile([P, CIN, PACK], BF16, name="grouped", align_bytes=64)
+            for k in quarters:
+                cols = slice(QUARTER * k, QUARTER * (k + 1))
+                nc.scalar.copy(out=grouped_w[g][:, cols, :], in_=raw_w[g][:, :, cols].rearrange("p j i -> p i j"))
+
+        def quantize_w(g):
+            nc.vector.quantize_mx(
+                out=w_codes[:, g, :].bitcast(E4M3), scales=w_scales[:, g, :],
+                in_=grouped_w[g][:].rearrange("p i j -> p (i j)"),
+            )
+
+        def dx_passes(b, t, groups):
+            if groups[0] == 0:
+                dx_acc[b, t] = acc_psum.tile([P, N], F32, name="acc")
+            rows = slice(P * t, P * (t + 1))
+            for g in groups:
                 nc.tensor.matmul_mx(
-                    out=T["p0", b, t][:],
-                    lhsT=cW[:, g, P * t : P * (t + 1)].bitcast(E4), lhsT_scale=sW[:, g, P * t : P * (t + 1)],
-                    rhs=cA[:, b, g, :].bitcast(E5), rhs_scale=sA[:, b, g, :],
+                    out=dx_acc[b, t][:],
+                    lhsT=w_codes[:, g, rows].bitcast(E4M3), lhsT_scale=w_scales[:, g, rows],
+                    rhs=dzc_codes[:, b, g, :].bitcast(E5M2), rhs_scale=dzc_scales[:, b, g, :],
                     start=(g == 0), stop=(g == G - 1),
                 )
 
-        def o0(b, t, eng="S"):
-            T["sb", b, t] = st0pool.tile([P, N], F32, name="sb")
-            copy_on(eng, T["sb", b, t][:], T["p0", b, t][:])
+        def dx_out(b, t, engine):
+            dx_rows = dx_pool.tile([P, N], F32, name="dx_rows")
+            copy_on(engine, dx_rows[:], dx_acc[b, t][:])
+            nc.sync.dma_start(out=out_0[b, P * t : P * (t + 1), :], in_=dx_rows[:])
 
-        def s0(b, t):
-            nc.sync.dma_start(out=out_0[b, P * t : P * (t + 1), :], in_=T["sb", b, t][:])
+        def dw_group(g, q):
+            j, half = divmod(q, 2)
+            rows = slice(P * j, P * (j + 1))
+            cols = slice(N * half, N * (half + 1))
+            dw_acc[g, q] = acc_psum.tile([P, N], F32, name="acc")
+            for b in range(B):
+                nc.tensor.matmul_mx(
+                    out=dw_acc[g, q][:],
+                    lhsT=dzt_codes[:, b, g, rows].bitcast(E5M2), lhsT_scale=dzt_scales[:, b, g, rows],
+                    rhs=x_codes[:, b, cols].bitcast(E4M3), rhs_scale=x_scales[:, b, cols],
+                    start=(b == 0), stop=(b == B - 1),
+                )
 
-        FN = {"gv": gv, "a1": a1, "sqrt": sqrt, "a2": a2, "L": L, "Lh": Lh, "maskh": maskh, "LX": LX, "LW": LW, "mask": mask, "scale": scale, "weave": weave,
-              "qa": qa, "turn": turn, "unturn": unturn, "qb": qb, "xt": xt, "xc": xc, "xq": xq, "wi": wi, "wq": wq,
-              "m1": m1, "o1": o1, "s1": s1, "m0": m0, "o0": o0, "s0": s0}
+        def dw_out(g, q):
+            j, half = divmod(q, 2)
+            if q % 4 == 0:
+                dw_rows[g] = dw_pool.tile([P, 2, CIN], F32, name="dw_rows")
+            nc.scalar.copy(out=dw_rows[g][:, j % 2, N * half : N * (half + 1)], in_=dw_acc[g, q][:])
+            if q % 4 == 3:
+                nc.sync.dma_start(out=dw_view[g][:, j - 1 : j + 1, :], in_=dw_rows[g][:])
+
         with tc.manual_schedule():
-            for step in RUN:
-                FN[step[0]](*step[1:])
+            load_slope_inputs()
+            load_chunk(0, pieces=2)
+            for g in range(3):
+                load_w(g)
+                load_chunk(g + 1)
+
+            mask(0, slice(0, PACK // 2))
+            slope_variance()
+            slope_sqrt()
+            mask(0, slice(PACK // 2, PACK))
+            slope_finish()
+
+            for s in range(G):
+                if s > 0:
+                    mask(s)
+                    quantize_w(s - 1)
+                    quantize_by_token(s - 1)
+                scale(s)
+                if s > 0:
+                    quantize_by_channel(s - 1)
+                weave(s)
+
+                weave_w(s, [0] if s == 0 else [0, 1, 2, 3])
+                if s == G - 1:
+                    turn_x(0)
+                turn(s)
+                unturn(s)
+                if s == 0:
+                    weave_w(s, [1, 2, 3])
+                else:
+                    for t in range(OPEN_TILES):
+                        dx_passes(0, t, [s - 1])
+
+                if s == 0:
+                    load_w(G - 1)
+                elif s == 1:
+                    load_x(0)
+                    load_chunk(G)
+                elif s == 2:
+                    load_x(1)
+                    load_chunk(G + 1)
+                    load_chunk(G + 2)
+                else:
+                    load_chunk(G + 3)
+
+            quantize_w(G - 1)
+            turn_x(1)
+            quantize_by_channel(G - 1)
+            quantize_x(0)
+            mask(G)
+            scale(G)
+            for t in range(OPEN_TILES):
+                dx_passes(0, t, [G - 1])
+                dx_out(0, t, "scalar")
+            turn(G)
+            unturn(G)
+            quantize_x(1)
+            quantize_by_token(G - 1)
+            quantize_by_token(G)
+            mask(G + 1)
+            scale(G + 1)
+            for t in range(OPEN_TILES, IT):
+                dx_passes(0, t, [0, 1, 2, 3])
+                dx_out(0, t, "scalar")
+
+            for g in range(G):
+                for q in range(2 * PACK):
+                    if q == PACK and g < G - 1:
+                        turn(G + g + 1)
+                        unturn(G + g + 1)
+                    dw_group(g, q)
+                    dw_out(g, q)
+                if g == 0:
+                    mask(G + 2)
+                    quantize_by_token(G + 1)
+                    scale(G + 2)
+                    weave(G)
+                elif g == 1:
+                    mask(G + 3)
+                    quantize_by_channel(G)
+                    quantize_by_token(G + 2)
+                    scale(G + 3)
+                    weave(G + 1)
+                elif g == 2:
+                    weave(G + 2)
+                    quantize_by_channel(G + 1)
+                    quantize_by_token(G + 3)
+                    weave(G + 3)
+                    quantize_by_channel(G + 2)
+                    quantize_by_channel(G + 3)
+
+            for t in range(IT):
+                dx_passes(1, t, [0, 1, 2, 3])
+                dx_out(1, t, "vector" if t % 2 == 1 else "scalar")

@@ -90,8 +90,8 @@ def tile_bottleneck_transformer_pb_v_kernel(
                 nc.scalar.copy(out=out, in_=in_)
 
         def load_slope_inputs():
-            nc.scalar.dma_start(out=var_bf[:].rearrange("p (g j) -> p g j", j=PACK), in_=scbn_v.rearrange("(g p j) -> p g j", p=P, j=PACK))
-            nc.scalar.dma_start(out=gain_bf[:].rearrange("p (g j) -> p g j", j=PACK), in_=scbn_g.rearrange("(g p j) -> p g j", p=P, j=PACK))
+            nc.sync.dma_start(out=var_bf[:].rearrange("p (g j) -> p g j", j=PACK), in_=scbn_v.rearrange("(g p j) -> p g j", p=P, j=PACK))
+            nc.sync.dma_start(out=gain_bf[:].rearrange("p (g j) -> p g j", j=PACK), in_=scbn_g.rearrange("(g p j) -> p g j", p=P, j=PACK))
 
         def load_chunk(s, pieces=1):
             b, g = divmod(s, G)
@@ -124,18 +124,22 @@ def tile_bottleneck_transformer_pb_v_kernel(
             nc.vector.tensor_tensor(out=rstd_fine[:], in0=rstd[:], in1=newton_c[:], op=ALU.mult)
             nc.vector.tensor_tensor(out=slope[:], in0=rstd_fine[:], in1=gain_bf[:], op=ALU.mult)
 
-        def mask(s, js=slice(0, PACK)):
-            nc.vector.scalar_tensor_tensor(
-                out=grad_tile[s][:, js, :], in0=z_tile[s][:, js, :], scalar=0.0, in1=grad_tile[s][:, js, :],
-                op0=ALU.is_gt, op1=ALU.mult,
-            )
+        def mask(s, pieces=1):
+            step = PACK // pieces
+            for j0 in range(0, PACK, step):
+                js = slice(j0, j0 + step)
+                nc.vector.scalar_tensor_tensor(
+                    out=grad_tile[s][:, js, :], in0=z_tile[s][:, js, :], scalar=0.0, in1=grad_tile[s][:, js, :],
+                    op0=ALU.is_gt, op1=ALU.mult,
+                )
 
         def scale(s):
             g = s % G
             dz_tile[s] = dz_pool.tile([P, PACK, N], BF16, name="dz_tile")
             for j in range(PACK):
                 nc.vector.tensor_scalar(
-                    out=dz_tile[s][:, j, :], in0=grad_tile[s][:, j, :],
+                    out=dz_tile[s][:, j, :].rearrange("p (u q e) -> p q u e", u=2, e=2),
+                    in0=grad_tile[s][:, j, :].rearrange("p (q u e) -> p q u e", u=2, e=2),
                     scalar1=slope[:, PACK * g + j : PACK * g + j + 1], scalar2=None, op0=ALU.mult,
                 )
 
@@ -156,8 +160,8 @@ def tile_bottleneck_transformer_pb_v_kernel(
                 turned[s, h] = turn_psum.tile([P, 2, 2, P], F32, name="turned")
                 for a in range(2):
                     for u in range(2):
-                        row = 2 * h + a
-                        nc.tensor.transpose(turned[s, h][:, a, u, :], words[:, WORDS * row + u : WORDS * (row + 1) : 2], ident[:])
+                        first = WORDS * (2 * h + a) + P * u
+                        nc.tensor.transpose(turned[s, h][:, a, u, :], words[:, first : first + P], ident[:])
 
         def unturn(s):
             by_token[s] = by_token_pool.tile([P, KP * PACK], BF16, name="by_token", align_bytes=64)
@@ -211,7 +215,7 @@ def tile_bottleneck_transformer_pb_v_kernel(
 
         def dx_out(b, t, engine):
             dx_rows = dx_pool.tile([P, N], F32, name="dx_rows")
-            copy_on(engine, dx_rows[:], dx_acc[b, t][:])
+            copy_on(engine, dx_rows[:].rearrange("p (q u e) -> p q u e", u=2, e=2), dx_acc[b, t][:].rearrange("p (u q e) -> p q u e", u=2, e=2))
             nc.sync.dma_start(out=out_0[b, P * t : P * (t + 1), :], in_=dx_rows[:])
 
         def dw_group(g, q):
@@ -241,16 +245,13 @@ def tile_bottleneck_transformer_pb_v_kernel(
             for g in range(3):
                 load_w(g)
                 load_chunk(g + 1)
-
-            mask(0, slice(0, PACK // 2))
             slope_variance()
             slope_sqrt()
-            mask(0, slice(PACK // 2, PACK))
             slope_finish()
 
             for s in range(G):
+                mask(s, pieces=2 if s == 0 else 1)
                 if s > 0:
-                    mask(s)
                     quantize_w(s - 1)
                     quantize_by_token(s - 1)
                 scale(s)

@@ -145,7 +145,9 @@ def tile_bottleneck_transformer_pb_v_kernel(
 
         def weave(s):
             by_channel[s] = by_channel_pool.tile([P, N, PACK], BF16, name="by_channel", align_bytes=64)
-            nc.vector.tensor_copy(out=by_channel[s][:], in_=dz_tile[s][:].rearrange("p j n -> p n j"))
+            nc.vector.tensor_copy(
+                out=by_channel[s][:].rearrange("p (c i) j -> p c j i", i=4), in_=dz_tile[s][:].rearrange("p j (c i) -> p c j i", i=4)
+            )
 
         def quantize_by_channel(s):
             b, g = divmod(s, G)
@@ -193,7 +195,10 @@ def tile_bottleneck_transformer_pb_v_kernel(
                 grouped_w[g] = grouped_pool.tile([P, CIN, PACK], BF16, name="grouped", align_bytes=64)
             for k in quarters:
                 cols = slice(QUARTER * k, QUARTER * (k + 1))
-                nc.scalar.copy(out=grouped_w[g][:, cols, :], in_=raw_w[g][:, :, cols].rearrange("p j i -> p i j"))
+                nc.scalar.copy(
+                    out=grouped_w[g][:, cols, :].rearrange("p (c i) j -> p c j i", i=4),
+                    in_=raw_w[g][:, :, cols].rearrange("p j (c i) -> p c j i", i=4),
+                )
 
         def quantize_w(g):
             nc.vector.quantize_mx(

@@ -22,6 +22,7 @@ G = COUT // KP
 IT = CIN // P
 WORDS = N // 2
 QUARTER = CIN // 4
+RUN = 4
 
 OPEN_TILES = 5
 
@@ -38,7 +39,7 @@ def tile_bottleneck_transformer_pb_v_kernel(
     z_view = z.rearrange("b (g p j) n -> b g p j n", p=P, j=PACK)
     grad_view = grad_out.rearrange("b (g p j) n -> b g p j n", p=P, j=PACK)
     w_view = sc_w.rearrange("(g p j) i -> g p j i", p=P, j=PACK)
-    x_view = x.rearrange("b (p t) n -> b p t n", t=IT)
+    x_view = x.rearrange("b (p v) n -> b p v n", v=IT)
     dw_view = out_1.rearrange("(g m j) i -> g m j i", m=P, j=PACK)
 
     with ExitStack() as ctx:
@@ -108,7 +109,7 @@ def tile_bottleneck_transformer_pb_v_kernel(
 
         def load_x(b):
             raw_x[b] = raw_pool.tile([P, IT * N], BF16, name="raw")
-            nc.sync.dma_start(out=raw_x[b][:].rearrange("p (t n) -> p t n", t=IT), in_=x_view[b])
+            nc.sync.dma_start(out=raw_x[b][:].rearrange("p (v n) -> p v n", v=IT), in_=x_view[b])
 
         def slope_variance():
             nc.vector.tensor_scalar(out=var_eps[:], in0=var_bf[:], scalar1=EPS, scalar2=None, op0=ALU.add)
@@ -143,10 +144,10 @@ def tile_bottleneck_transformer_pb_v_kernel(
                     scalar1=slope[:, PACK * g + j : PACK * g + j + 1], scalar2=None, op0=ALU.mult,
                 )
 
-        def weave(s):
+        def interleave_dz(s):
             by_channel[s] = by_channel_pool.tile([P, N, PACK], BF16, name="by_channel", align_bytes=64)
             nc.vector.tensor_copy(
-                out=by_channel[s][:].rearrange("p (c i) j -> p c j i", i=4), in_=dz_tile[s][:].rearrange("p j (c i) -> p c j i", i=4)
+                out=by_channel[s][:].rearrange("p (c r) j -> p c j r", r=RUN), in_=dz_tile[s][:].rearrange("p j (c r) -> p c j r", r=RUN)
             )
 
         def quantize_by_channel(s):
@@ -156,7 +157,7 @@ def tile_bottleneck_transformer_pb_v_kernel(
                 in_=by_channel[s][:].rearrange("p n j -> p (n j)"),
             )
 
-        def turn(s):
+        def transpose_dz(s):
             words = dz_tile[s][:].rearrange("p j n -> p (j n)").bitcast(F32)
             for h in range(2):
                 turned[s, h] = turn_psum.tile([P, 2, 2, P], F32, name="turned")
@@ -165,7 +166,7 @@ def tile_bottleneck_transformer_pb_v_kernel(
                         first = WORDS * (2 * h + a) + P * u
                         nc.tensor.transpose(turned[s, h][:, a, u, :], words[:, first : first + P], ident[:])
 
-        def unturn(s):
+        def collect_dz(s):
             by_token[s] = by_token_pool.tile([P, KP * PACK], BF16, name="by_token", align_bytes=64)
             dst = by_token[s][:].bitcast(F32).rearrange("p (j m u) -> p j m u", j=PACK, u=2)
             for h in range(2):
@@ -175,11 +176,12 @@ def tile_bottleneck_transformer_pb_v_kernel(
             b, g = divmod(s, G)
             nc.vector.quantize_mx(out=dzt_codes[:, b, g, :].bitcast(E5M2), scales=dzt_scales[:, b, g, :], in_=by_token[s][:])
 
-        def turn_x(b):
+        def transpose_x(b, banks):
             words = raw_x[b][:].bitcast(F32)
-            grouped_x[b] = grouped_pool.tile([P, CIN * PACK], BF16, name="grouped", align_bytes=64)
-            dst = grouped_x[b][:].bitcast(F32).rearrange("p (m t u) -> p m t u", t=IT, u=2)
-            for h in range(IT // 2):
+            if banks[0] == 0:
+                grouped_x[b] = grouped_pool.tile([P, CIN * PACK], BF16, name="grouped", align_bytes=64)
+            dst = grouped_x[b][:].bitcast(F32).rearrange("p (m v u) -> p m v u", v=IT, u=2)
+            for h in banks:
                 turned_x = turn_psum.tile([P, 2, 2, P], F32, name="turned")
                 for a in range(2):
                     for u in range(2):
@@ -190,14 +192,14 @@ def tile_bottleneck_transformer_pb_v_kernel(
         def quantize_x(b):
             nc.vector.quantize_mx(out=x_codes[:, b, :].bitcast(E4M3), scales=x_scales[:, b, :], in_=grouped_x[b][:])
 
-        def weave_w(g, quarters):
+        def interleave_w(g, quarters):
             if quarters[0] == 0:
                 grouped_w[g] = grouped_pool.tile([P, CIN, PACK], BF16, name="grouped", align_bytes=64)
-            for k in quarters:
-                cols = slice(QUARTER * k, QUARTER * (k + 1))
+            for quarter in quarters:
+                cols = slice(QUARTER * quarter, QUARTER * (quarter + 1))
                 nc.scalar.copy(
-                    out=grouped_w[g][:, cols, :].rearrange("p (c i) j -> p c j i", i=4),
-                    in_=raw_w[g][:, :, cols].rearrange("p j (c i) -> p c j i", i=4),
+                    out=grouped_w[g][:, cols, :].rearrange("p (c r) j -> p c j r", r=RUN),
+                    in_=raw_w[g][:, :, cols].rearrange("p j (c r) -> p c j r", r=RUN),
                 )
 
         def quantize_w(g):
@@ -223,31 +225,33 @@ def tile_bottleneck_transformer_pb_v_kernel(
             copy_on(engine, dx_rows[:].rearrange("p (q u e) -> p q u e", u=2, e=2), dx_acc[b, t][:].rearrange("p (u q e) -> p q u e", u=2, e=2))
             nc.sync.dma_start(out=out_0[b, P * t : P * (t + 1), :], in_=dx_rows[:])
 
-        def dw_group(g, q):
-            j, half = divmod(q, 2)
+        def dw_tile(g, y):
+            j, side = divmod(y, 2)
             rows = slice(P * j, P * (j + 1))
-            cols = slice(N * half, N * (half + 1))
-            dw_acc[g, q] = acc_psum.tile([P, N], F32, name="acc")
+            cols = slice(N * side, N * (side + 1))
+            dw_acc[g, y] = acc_psum.tile([P, N], F32, name="acc")
             for b in range(B):
                 nc.tensor.matmul_mx(
-                    out=dw_acc[g, q][:],
+                    out=dw_acc[g, y][:],
                     lhsT=dzt_codes[:, b, g, rows].bitcast(E5M2), lhsT_scale=dzt_scales[:, b, g, rows],
                     rhs=x_codes[:, b, cols].bitcast(E4M3), rhs_scale=x_scales[:, b, cols],
                     start=(b == 0), stop=(b == B - 1),
                 )
 
-        def dw_out(g, q):
-            j, half = divmod(q, 2)
-            if q % 4 == 0:
+        def dw_out(g, y):
+            j, side = divmod(y, 2)
+            if y % 4 == 0:
                 dw_rows[g] = dw_pool.tile([P, 2, CIN], F32, name="dw_rows")
-            nc.scalar.copy(out=dw_rows[g][:, j % 2, N * half : N * (half + 1)], in_=dw_acc[g, q][:])
-            if q % 4 == 3:
+            nc.scalar.copy(out=dw_rows[g][:, j % 2, N * side : N * (side + 1)], in_=dw_acc[g, y][:])
+            if y % 4 == 3:
                 nc.sync.dma_start(out=dw_view[g][:, j - 1 : j + 1, :], in_=dw_rows[g][:])
 
+        all_groups = list(range(G))
+        all_quarters = list(range(CIN // QUARTER))
         with tc.manual_schedule():
             load_slope_inputs()
             load_chunk(0, pieces=2)
-            for g in range(3):
+            for g in range(G - 1):
                 load_w(g)
                 load_chunk(g + 1)
             slope_variance()
@@ -255,24 +259,46 @@ def tile_bottleneck_transformer_pb_v_kernel(
             slope_finish()
 
             for s in range(G):
-                mask(s, pieces=2 if s == 0 else 1)
-                if s > 0:
-                    quantize_w(s - 1)
-                    quantize_by_token(s - 1)
-                scale(s)
-                if s > 0:
-                    quantize_by_channel(s - 1)
-                weave(s)
-
-                weave_w(s, [0] if s == 0 else [0, 1, 2, 3])
-                if s == G - 1:
-                    turn_x(0)
-                turn(s)
-                unturn(s)
                 if s == 0:
-                    weave_w(s, [1, 2, 3])
+                    mask(0, pieces=2)
+                    scale(0)
+                elif s == 1:
+                    mask(1)
+                    quantize_by_token(0)
+                    scale(1)
+                    quantize_by_channel(0)
+                    quantize_w(0)
+                elif s == 2:
+                    quantize_w(1)
+                    quantize_by_token(1)
+                    mask(2)
+                    scale(2)
+                    quantize_by_channel(1)
                 else:
-                    for t in range(OPEN_TILES):
+                    mask(3)
+                    quantize_w(2)
+                    quantize_by_token(2)
+                    scale(3)
+                    quantize_by_channel(2)
+                interleave_dz(s)
+
+                interleave_w(s, all_quarters[:1] if s == 0 else all_quarters)
+                if s < G - 1:
+                    transpose_dz(s)
+                    collect_dz(s)
+                    if s == 0:
+                        interleave_w(s, all_quarters[1:])
+                    else:
+                        for t in range(OPEN_TILES):
+                            dx_passes(0, t, [s - 1])
+                else:
+                    transpose_x(0, [0, 1, 2])
+                    for t in range(3):
+                        dx_passes(0, t, [s - 1])
+                    transpose_x(0, [3])
+                    transpose_dz(s)
+                    collect_dz(s)
+                    for t in range(3, OPEN_TILES):
                         dx_passes(0, t, [s - 1])
 
                 if s == 0:
@@ -288,51 +314,55 @@ def tile_bottleneck_transformer_pb_v_kernel(
                     load_chunk(G + 3)
 
             quantize_w(G - 1)
-            turn_x(1)
             quantize_by_channel(G - 1)
+            transpose_x(1, [0, 1])
+            for t in range(2):
+                dx_passes(0, t, [G - 1])
+            transpose_x(1, [2, 3])
+            for t in range(2, OPEN_TILES):
+                dx_passes(0, t, [G - 1])
             quantize_x(0)
             mask(G)
             scale(G)
             for t in range(OPEN_TILES):
-                dx_passes(0, t, [G - 1])
                 dx_out(0, t, "scalar")
-            turn(G)
-            unturn(G)
+            transpose_dz(G)
+            collect_dz(G)
             quantize_x(1)
             quantize_by_token(G - 1)
-            quantize_by_token(G)
             mask(G + 1)
+            quantize_by_token(G)
             scale(G + 1)
             for t in range(OPEN_TILES, IT):
-                dx_passes(0, t, [0, 1, 2, 3])
+                dx_passes(0, t, all_groups)
                 dx_out(0, t, "scalar")
 
             for g in range(G):
-                for q in range(2 * PACK):
-                    if q == PACK and g < G - 1:
-                        turn(G + g + 1)
-                        unturn(G + g + 1)
-                    dw_group(g, q)
-                    dw_out(g, q)
+                for y in range(2 * PACK):
+                    if y == PACK and g < G - 1:
+                        transpose_dz(G + g + 1)
+                        collect_dz(G + g + 1)
+                    dw_tile(g, y)
+                    dw_out(g, y)
                 if g == 0:
                     mask(G + 2)
                     quantize_by_token(G + 1)
                     scale(G + 2)
-                    weave(G)
+                    interleave_dz(G)
                 elif g == 1:
                     mask(G + 3)
                     quantize_by_channel(G)
                     quantize_by_token(G + 2)
                     scale(G + 3)
-                    weave(G + 1)
+                    interleave_dz(G + 1)
                 elif g == 2:
-                    weave(G + 2)
+                    interleave_dz(G + 2)
                     quantize_by_channel(G + 1)
                     quantize_by_token(G + 3)
-                    weave(G + 3)
+                    interleave_dz(G + 3)
                     quantize_by_channel(G + 2)
                     quantize_by_channel(G + 3)
 
             for t in range(IT):
-                dx_passes(1, t, [0, 1, 2, 3])
+                dx_passes(1, t, all_groups)
                 dx_out(1, t, "vector" if t % 2 == 1 else "scalar")

from contextlib import ExitStack

import concourse.mybir as mybir
from concourse.masks import make_identity

B, CIN, COUT, N = 2, 1024, 2048, 512
EPS = 1e-5

F32 = mybir.dt.float32
BF16 = mybir.dt.bfloat16
U32 = mybir.dt.uint32
U8 = mybir.dt.uint8
E4M3 = mybir.dt.float8_e4m3fn_x4
E5M2 = mybir.dt.float8_e5m2_x4
ALU = mybir.AluOpType
ACT = mybir.ActivationFunctionType

P = 128
PACK = 4
KP = P * PACK
G = COUT // KP
IT = CIN // P
WORDS = N // 2
QUARTER = CIN // 4
RUN = 4

OPEN_TILES = 5

FLOPS = 2 * 2 * COUT * CIN * B * N
BYTES = 2 * (B * CIN * N + COUT * CIN + B * COUT * N + 2 * COUT) + 4 * (B * COUT * N + B * CIN * N + COUT * CIN)


def tile_bottleneck_transformer_pb_v_kernel(
    tc, h_attn, x, conv3_w, bn3_g, bn3_b, bn3_m, bn3_v, sc_w, sc_b,
    scbn_g, scbn_b, scbn_m, scbn_v, z, grad_out, out_0, out_1,
):
    nc = tc.nc

    z_view = z.rearrange("b (g p j) n -> b g p j n", p=P, j=PACK)
    grad_view = grad_out.rearrange("b (g p j) n -> b g p j n", p=P, j=PACK)
    w_view = sc_w.rearrange("(g p j) i -> g p j i", p=P, j=PACK)
    x_view = x.rearrange("b (p v) n -> b p v n", v=IT)
    dw_view = out_1.rearrange("(g m j) i -> g m j i", m=P, j=PACK)

    with ExitStack() as ctx:
        const = ctx.enter_context(tc.tile_pool(name="const", bufs=1))
        keep = ctx.enter_context(tc.tile_pool(name="keep", bufs=1))
        z_pool = ctx.enter_context(tc.tile_pool(name="z_pool", bufs=4))
        grad_pool = ctx.enter_context(tc.tile_pool(name="grad_pool", bufs=4))
        dz_pool = ctx.enter_context(tc.tile_pool(name="dz_pool", bufs=4))
        by_channel_pool = ctx.enter_context(tc.tile_pool(name="by_channel_pool", bufs=2))
        by_token_pool = ctx.enter_context(tc.tile_pool(name="by_token_pool", bufs=2))
        grouped_pool = ctx.enter_context(tc.tile_pool(name="grouped_pool", bufs=2))
        raw_pool = ctx.enter_context(tc.tile_pool(name="raw_pool", bufs=3))
        dw_pool = ctx.enter_context(tc.tile_pool(name="dw_pool", bufs=3))
        dx_pool = ctx.enter_context(tc.tile_pool(name="dx_pool", bufs=8))
        turn_psum = ctx.enter_context(tc.psum_pool(name="turn_psum", bufs=8 - OPEN_TILES))
        acc_psum = ctx.enter_context(tc.psum_pool(name="acc_psum", bufs=OPEN_TILES))

        dzc_codes = keep.tile([P, B, G, N], U32, name="dzc_codes", align_bytes=64)
        dzc_scales = keep.tile([P, B, G, N], U8, name="dzc_scales", align_bytes=64)
        dzt_codes = keep.tile([P, B, G, KP], U32, name="dzt_codes", align_bytes=64)
        dzt_scales = keep.tile([P, B, G, KP], U8, name="dzt_scales", align_bytes=64)
        w_codes = keep.tile([P, G, CIN], U32, name="w_codes", align_bytes=64)
        w_scales = keep.tile([P, G, CIN], U8, name="w_scales", align_bytes=64)
        x_codes = keep.tile([P, B, CIN], U32, name="x_codes", align_bytes=64)
        x_scales = keep.tile([P, B, CIN], U8, name="x_scales", align_bytes=64)

        ident = const.tile([P, P], F32, name="ident")
        make_identity(nc, ident[:])

        gain_bf = const.tile([P, G * PACK], BF16, name="gain_bf")
        var_bf = const.tile([P, G * PACK], BF16, name="var_bf")
        var_eps = const.tile([P, G * PACK], F32, name="var_eps")
        std = const.tile([P, G * PACK], F32, name="std")
        rstd = const.tile([P, G * PACK], F32, name="rstd")
        newton_a = const.tile([P, G * PACK], F32, name="newton_a")
        newton_b = const.tile([P, G * PACK], F32, name="newton_b")
        newton_c = const.tile([P, G * PACK], F32, name="newton_c")
        rstd_fine = const.tile([P, G * PACK], F32, name="rstd_fine")
        slope = const.tile([P, G * PACK], F32, name="slope")

        z_tile, grad_tile, dz_tile, by_channel, by_token = {}, {}, {}, {}, {}
        raw_w, raw_x, grouped_w, grouped_x = {}, {}, {}, {}
        turned, dx_acc, dw_acc, dw_rows = {}, {}, {}, {}

        def copy_on(engine, out, in_):
            if engine == "vector":
                nc.vector.tensor_copy(out=out, in_=in_)
            else:
                nc.scalar.copy(out=out, in_=in_)

        def load_slope_inputs():
            nc.sync.dma_start(out=var_bf[:].rearrange("p (g j) -> p g j", j=PACK), in_=scbn_v.rearrange("(g p j) -> p g j", p=P, j=PACK))
            nc.sync.dma_start(out=gain_bf[:].rearrange("p (g j) -> p g j", j=PACK), in_=scbn_g.rearrange("(g p j) -> p g j", p=P, j=PACK))

        def load_chunk(s, pieces=1):
            b, g = divmod(s, G)
            z_tile[s] = z_pool.tile([P, PACK, N], F32, name="z_tile")
            grad_tile[s] = grad_pool.tile([P, PACK, N], BF16, name="grad_tile")
            step = PACK // pieces
            for j0 in range(0, PACK, step):
                nc.sync.dma_start(out=z_tile[s][:, j0 : j0 + step, :], in_=z_view[b, g][:, j0 : j0 + step, :])
                nc.sync.dma_start(out=grad_tile[s][:, j0 : j0 + step, :], in_=grad_view[b, g][:, j0 : j0 + step, :])

        def load_w(g):
            raw_w[g] = raw_pool.tile([P, PACK, CIN], BF16, name="raw")
            nc.sync.dma_start(out=raw_w[g][:], in_=w_view[g])

        def load_x(b):
            raw_x[b] = raw_pool.tile([P, IT * N], BF16, name="raw")
            nc.sync.dma_start(out=raw_x[b][:].rearrange("p (v n) -> p v n", v=IT), in_=x_view[b])

        def slope_variance():
            nc.vector.tensor_scalar(out=var_eps[:], in0=var_bf[:], scalar1=EPS, scalar2=None, op0=ALU.add)

        def slope_sqrt():
            nc.scalar.activation(out=std[:], in_=var_eps[:], func=ACT.Sqrt)

        def slope_finish():
            nc.vector.reciprocal(out=rstd[:], in_=std[:])
            nc.vector.tensor_tensor(out=newton_a[:], in0=rstd[:], in1=rstd[:], op=ALU.mult)
            nc.vector.tensor_tensor(out=newton_b[:], in0=newton_a[:], in1=var_eps[:], op=ALU.mult)
            nc.vector.tensor_scalar(out=newton_c[:], in0=newton_b[:], scalar1=-0.5, scalar2=1.5, op0=ALU.mult, op1=ALU.add)
            nc.vector.tensor_tensor(out=rstd_fine[:], in0=rstd[:], in1=newton_c[:], op=ALU.mult)
            nc.vector.tensor_tensor(out=slope[:], in0=rstd_fine[:], in1=gain_bf[:], op=ALU.mult)

        def mask(s, pieces=1):
            step = PACK // pieces
            for j0 in range(0, PACK, step):
                js = slice(j0, j0 + step)
                nc.vector.scalar_tensor_tensor(
                    out=grad_tile[s][:, js, :], in0=z_tile[s][:, js, :], scalar=0.0, in1=grad_tile[s][:, js, :],
                    op0=ALU.is_gt, op1=ALU.mult,
                )

        def scale(s):
            g = s % G
            dz_tile[s] = dz_pool.tile([P, PACK, N], BF16, name="dz_tile")
            for j in range(PACK):
                nc.vector.tensor_scalar(
                    out=dz_tile[s][:, j, :].rearrange("p (u q e) -> p q u e", u=2, e=2),
                    in0=grad_tile[s][:, j, :].rearrange("p (q u e) -> p q u e", u=2, e=2),
                    scalar1=slope[:, PACK * g + j : PACK * g + j + 1], scalar2=None, op0=ALU.mult,
                )

        def interleave_dz(s):
            by_channel[s] = by_channel_pool.tile([P, N, PACK], BF16, name="by_channel", align_bytes=64)
            nc.vector.tensor_copy(
                out=by_channel[s][:].rearrange("p (c r) j -> p c j r", r=RUN), in_=dz_tile[s][:].rearrange("p j (c r) -> p c j r", r=RUN)
            )

        def quantize_by_channel(s):
            b, g = divmod(s, G)
            nc.vector.quantize_mx(
                out=dzc_codes[:, b, g, :].bitcast(E5M2), scales=dzc_scales[:, b, g, :],
                in_=by_channel[s][:].rearrange("p n j -> p (n j)"),
            )

        def transpose_dz(s):
            words = dz_tile[s][:].rearrange("p j n -> p (j n)").bitcast(F32)
            for h in range(2):
                turned[s, h] = turn_psum.tile([P, 2, 2, P], F32, name="turned")
                for a in range(2):
                    for u in range(2):
                        first = WORDS * (2 * h + a) + P * u
                        nc.tensor.transpose(turned[s, h][:, a, u, :], words[:, first : first + P], ident[:])

        def collect_dz(s):
            by_token[s] = by_token_pool.tile([P, KP * PACK], BF16, name="by_token", align_bytes=64)
            dst = by_token[s][:].bitcast(F32).rearrange("p (j m u) -> p j m u", j=PACK, u=2)
            for h in range(2):
                nc.scalar.copy(out=dst[:, 2 * h : 2 * h + 2, :, :], in_=turned[s, h][:].rearrange("p a u m -> p a m u"))

        def quantize_by_token(s):
            b, g = divmod(s, G)
            nc.vector.quantize_mx(out=dzt_codes[:, b, g, :].bitcast(E5M2), scales=dzt_scales[:, b, g, :], in_=by_token[s][:])

        def transpose_x(b, banks):
            words = raw_x[b][:].bitcast(F32)
            if banks[0] == 0:
                grouped_x[b] = grouped_pool.tile([P, CIN * PACK], BF16, name="grouped", align_bytes=64)
            dst = grouped_x[b][:].bitcast(F32).rearrange("p (m v u) -> p m v u", v=IT, u=2)
            for h in banks:
                turned_x = turn_psum.tile([P, 2, 2, P], F32, name="turned")
                for a in range(2):
                    for u in range(2):
                        row = 2 * h + a
                        nc.tensor.transpose(turned_x[:, a, u, :], words[:, WORDS * row + u : WORDS * (row + 1) : 2], ident[:])
                nc.scalar.copy(out=dst[:, :, 2 * h : 2 * h + 2, :], in_=turned_x[:].rearrange("p a u m -> p m a u"))

        def quantize_x(b):
            nc.vector.quantize_mx(out=x_codes[:, b, :].bitcast(E4M3), scales=x_scales[:, b, :], in_=grouped_x[b][:])

        def interleave_w(g, quarters):
            if quarters[0] == 0:
                grouped_w[g] = grouped_pool.tile([P, CIN, PACK], BF16, name="grouped", align_bytes=64)
            for quarter in quarters:
                cols = slice(QUARTER * quarter, QUARTER * (quarter + 1))
                nc.scalar.copy(
                    out=grouped_w[g][:, cols, :].rearrange("p (c r) j -> p c j r", r=RUN),
                    in_=raw_w[g][:, :, cols].rearrange("p j (c r) -> p c j r", r=RUN),
                )

        def quantize_w(g):
            nc.vector.quantize_mx(
                out=w_codes[:, g, :].bitcast(E4M3), scales=w_scales[:, g, :],
                in_=grouped_w[g][:].rearrange("p i j -> p (i j)"),
            )

        def dx_passes(b, t, groups):
            if groups[0] == 0:
                dx_acc[b, t] = acc_psum.tile([P, N], F32, name="acc")
            rows = slice(P * t, P * (t + 1))
            for g in groups:
                nc.tensor.matmul_mx(
                    out=dx_acc[b, t][:],
                    lhsT=w_codes[:, g, rows].bitcast(E4M3), lhsT_scale=w_scales[:, g, rows],
                    rhs=dzc_codes[:, b, g, :].bitcast(E5M2), rhs_scale=dzc_scales[:, b, g, :],
                    start=(g == 0), stop=(g == G - 1),
                )

        def dx_out(b, t, engine):
            dx_rows = dx_pool.tile([P, N], F32, name="dx_rows")
            copy_on(engine, dx_rows[:].rearrange("p (q u e) -> p q u e", u=2, e=2), dx_acc[b, t][:].rearrange("p (u q e) -> p q u e", u=2, e=2))
            nc.sync.dma_start(out=out_0[b, P * t : P * (t + 1), :], in_=dx_rows[:])

        def dw_tile(g, y):
            j, side = divmod(y, 2)
            rows = slice(P * j, P * (j + 1))
            cols = slice(N * side, N * (side + 1))
            dw_acc[g, y] = acc_psum.tile([P, N], F32, name="acc")
            for b in range(B):
                nc.tensor.matmul_mx(
                    out=dw_acc[g, y][:],
                    lhsT=dzt_codes[:, b, g, rows].bitcast(E5M2), lhsT_scale=dzt_scales[:, b, g, rows],
                    rhs=x_codes[:, b, cols].bitcast(E4M3), rhs_scale=x_scales[:, b, cols],
                    start=(b == 0), stop=(b == B - 1),
                )

        def dw_out(g, y):
            j, side = divmod(y, 2)
            if y % 4 == 0:
                dw_rows[g] = dw_pool.tile([P, 2, CIN], F32, name="dw_rows")
            nc.scalar.copy(out=dw_rows[g][:, j % 2, N * side : N * (side + 1)], in_=dw_acc[g, y][:])
            if y % 4 == 3:
                nc.sync.dma_start(out=dw_view[g][:, j - 1 : j + 1, :], in_=dw_rows[g][:])

        all_groups = list(range(G))
        all_quarters = list(range(CIN // QUARTER))
        with tc.manual_schedule():
            load_slope_inputs()
            load_chunk(0, pieces=2)
            for g in range(G - 1):
                load_w(g)
                load_chunk(g + 1)
            slope_variance()
            slope_sqrt()
            slope_finish()

            for s in range(G):
                if s == 0:
                    mask(0, pieces=2)
                    scale(0)
                elif s == 1:
                    mask(1)
                    quantize_by_token(0)
                    scale(1)
                    quantize_by_channel(0)
                    quantize_w(0)
                elif s == 2:
                    quantize_w(1)
                    quantize_by_token(1)
                    mask(2)
                    scale(2)
                    quantize_by_channel(1)
                else:
                    mask(3)
                    quantize_w(2)
                    quantize_by_token(2)
                    scale(3)
                    quantize_by_channel(2)
                interleave_dz(s)

                interleave_w(s, all_quarters[:1] if s == 0 else all_quarters)
                if s < G - 1:
                    transpose_dz(s)
                    collect_dz(s)
                    if s == 0:
                        interleave_w(s, all_quarters[1:])
                    else:
                        for t in range(OPEN_TILES):
                            dx_passes(0, t, [s - 1])
                else:
                    transpose_x(0, [0, 1, 2])
                    for t in range(3):
                        dx_passes(0, t, [s - 1])
                    transpose_x(0, [3])
                    transpose_dz(s)
                    collect_dz(s)
                    for t in range(3, OPEN_TILES):
                        dx_passes(0, t, [s - 1])

                if s == 0:
                    load_w(G - 1)
                elif s == 1:
                    load_x(0)
                    load_chunk(G)
                elif s == 2:
                    load_x(1)
                    load_chunk(G + 1)
                    load_chunk(G + 2)
                else:
                    load_chunk(G + 3)

            quantize_w(G - 1)
            quantize_by_channel(G - 1)
            transpose_x(1, [0, 1])
            for t in range(2):
                dx_passes(0, t, [G - 1])
            transpose_x(1, [2, 3])
            for t in range(2, OPEN_TILES):
                dx_passes(0, t, [G - 1])
            quantize_x(0)
            mask(G)
            scale(G)
            for t in range(OPEN_TILES):
                dx_out(0, t, "scalar")
            transpose_dz(G)
            collect_dz(G)
            quantize_x(1)
            quantize_by_token(G - 1)
            mask(G + 1)
            quantize_by_token(G)
            scale(G + 1)
            for t in range(OPEN_TILES, IT):
                dx_passes(0, t, all_groups)
                dx_out(0, t, "scalar")

            for g in range(G):
                for y in range(2 * PACK):
                    if y == PACK and g < G - 1:
                        transpose_dz(G + g + 1)
                        collect_dz(G + g + 1)
                    dw_tile(g, y)
                    dw_out(g, y)
                if g == 0:
                    mask(G + 2)
                    quantize_by_token(G + 1)
                    scale(G + 2)
                    interleave_dz(G)
                elif g == 1:
                    mask(G + 3)
                    quantize_by_channel(G)
                    quantize_by_token(G + 2)
                    scale(G + 3)
                    interleave_dz(G + 1)
                elif g == 2:
                    interleave_dz(G + 2)
                    quantize_by_channel(G + 1)
                    quantize_by_token(G + 3)
                    interleave_dz(G + 3)
                    quantize_by_channel(G + 2)
                    quantize_by_channel(G + 3)

            for t in range(IT):
                dx_passes(1, t, all_groups)
                dx_out(1, t, "vector" if t % 2 == 1 else "scalar")
